import numpy as np
import ml_dtypes


def mxq(x, axis, fmt="e4m3"):
    dtype, down = {"e4m3": (ml_dtypes.float8_e4m3fn, 7), "e5m2": (ml_dtypes.float8_e5m2, 14)}[fmt]
    v = np.moveaxis(np.asarray(x, np.float32).astype(ml_dtypes.bfloat16).astype(np.float64), axis, -1)
    blocks = v.reshape(v.shape[:-1] + (-1, 32))
    amax = np.abs(blocks).max(-1, keepdims=True)
    byte = np.maximum(np.where(amax > 0, np.frexp(amax)[1] - 1 + 127, 0) - down, 1)
    scale = np.exp2(byte - 127.0)
    codes = (blocks / scale).astype(np.float32).astype(dtype).astype(np.float64)
    return np.moveaxis((codes * scale).reshape(v.shape), -1, axis)


WIDE = False


def mx_kscale(k):
    if not WIDE:
        return np.ones(k)
    levels = np.array([10, -10, 5, -5, 0])
    a = np.random.permutation(np.resize(levels, k // 512 * 4)).reshape(k // 512, 4)
    idx = np.arange(k)
    return np.exp2(a[idx // 512, idx % 128 // 32])


BF16 = ml_dtypes.bfloat16


def bf(x):
    return np.asarray(x, np.float32).astype(BF16)


def f64(x):
    return np.asarray(x).astype(np.float64)


N, T, B, C, H = 256, 4, 8, 512, 128
N3 = T * N
O = H + H


def sigmoid(v):
    return 1.0 / (1.0 + np.exp(-v))


def setup_inputs():
    s, t = mx_kscale(N3), mx_kscale(C)
    return {"x": bf(np.random.standard_normal((N3, B, C)) * s[:, None, None] * t[None, None, :]),
            "A": bf(np.random.standard_normal((N3, N3)) / np.sqrt(N3) / s[None, :]),
            "W0": bf(np.random.standard_normal((O, C)) / np.sqrt(C) / t[None, :]),
            "b0": bf(np.random.standard_normal(O) * 0.3)}


def reference(x, A, W0, b0):
    h = f64(x).transpose(1, 2, 0)
    g = mxq(h, 2, "e4m3") @ mxq(f64(A), 1, "e4m3").T
    y = (mxq(f64(W0), 1, "e4m3") @ mxq(g, 1, "e4m3")) + f64(b0)[None, :, None]
    h1 = y[:, :H] * sigmoid(y[:, H:])
    return h1.transpose(2, 0, 1)

@@ -1,0 +1,269 @@
+from contextlib import ExitStack
+
+import concourse.mybir as mybir
+from concourse.masks import make_identity
+
+F32 = mybir.dt.float32
+BF16 = mybir.dt.bfloat16
+U32 = mybir.dt.uint32
+U8 = mybir.dt.uint8
+FP8X4 = mybir.dt.float8_e4m3fn_x4
+ACT = mybir.ActivationFunctionType
+ALU = mybir.AluOpType
+
+P = 128
+PACK = 4
+NODES = 1024
+BATCH = 8
+CHANNELS = 512
+HIDDEN = 128
+
+PASSES = NODES // (P * PACK)
+HALF = 512
+HALVES = NODES // HALF
+BLOCKS = HALF // P
+UNITS = BATCH * HALVES
+PIECES = BATCH * PASSES
+
+FLOPS = 2 * BATCH * CHANNELS * NODES * NODES + 2 * BATCH * 2 * HIDDEN * CHANNELS * NODES
+
+
+def tile_stsgcm_pa_t_kernel(tc, x, A, W0, b0, out):
+    nc = tc.nc
+    with ExitStack() as ctx:
+        ctx.enter_context(tc.manual_schedule())
+
+        const = ctx.enter_context(tc.tile_pool(name="const", bufs=1))
+        x_keep = ctx.enter_context(tc.tile_pool(name="x_keep", bufs=PIECES))
+        a_load = ctx.enter_context(tc.tile_pool(name="a_load", bufs=HALVES * BLOCKS))
+        a_keep = ctx.enter_context(tc.tile_pool(name="a_keep", bufs=HALVES))
+        x_stage = ctx.enter_context(tc.tile_pool(name="x_stage", bufs=3))
+        g_stage = ctx.enter_context(tc.tile_pool(name="g_stage", bufs=3))
+        glu = ctx.enter_context(tc.tile_pool(name="glu", bufs=4))
+        psum_g = ctx.enter_context(tc.psum_pool(name="psum_g", bufs=4))
+        psum_y = ctx.enter_context(tc.psum_pool(name="psum_y", bufs=2))
+        psum_t = ctx.enter_context(tc.psum_pool(name="psum_t", bufs=2))
+
+        ident_f32 = const.tile([P, P], F32)
+        make_identity(nc, ident_f32[:])
+        ident_bf16 = const.tile([P, P], BF16)
+        make_identity(nc, ident_bf16[:])
+        bias_rows = const.tile([P, P], BF16)
+        nc.vector.memset(bias_rows[:], 0.0)
+        zero_col = const.tile([P, 1], F32)
+        nc.vector.memset(zero_col[:], 0.0)
+        half_col = const.tile([P, 1], F32)
+        nc.scalar.activation(out=half_col[:], in_=zero_col[:], func=ACT.Sigmoid)
+
+        w_raw = const.tile([P, 2, CHANNELS], BF16)
+        nc.sync.dma_start(out=w_raw[:], in_=W0.rearrange("(h o) c -> o h c", h=2))
+        nc.sync.dma_start(out=bias_rows[0:2, :], in_=b0.rearrange("(h j) -> h j", h=2))
+
+        x_raw = {}
+
+        def load_x(b):
+            for s in range(PASSES):
+                x_piece = x_keep.tile([P, PACK, CHANNELS], BF16)
+                for u in range(2):
+                    first = s * P * PACK + u * 2 * P
+                    nc.sync.dma_start(
+                        out=x_piece[:, 2 * u : 2 * u + 2, :],
+                        in_=x[first : first + 2 * P, b, :].rearrange("(p e) c -> p e c", e=2),
+                    )
+                x_raw[PASSES * b + s] = x_piece
+
+        load_x(0)
+        a_raw = []
+        for block in range(HALVES * BLOCKS):
+            a_rows = a_load.tile([P, NODES], BF16)
+            nc.sync.dma_start(out=a_rows[:], in_=A[block * P : (block + 1) * P, :])
+            a_raw.append(a_rows)
+        for b in range(1, BATCH):
+            load_x(b)
+
+        w_grouped = const.tile([P, 2 * HIDDEN, PACK], BF16, align_bytes=64)
+        for h in range(2):
+            w_bank = psum_t.tile([P, PACK, P], BF16, tag="t")
+            for t in range(PACK):
+                nc.tensor.transpose(
+                    out=w_bank[:, t, :], in_=w_raw[:, h, t * P : (t + 1) * P], identity=ident_bf16[:]
+                )
+            nc.vector.tensor_copy(
+                out=w_grouped[:, h * HIDDEN : (h + 1) * HIDDEN, :],
+                in_=w_bank[:].rearrange("p t o -> p o t"),
+            )
+        bias_bank = psum_y.tile([P, P], BF16, tag="y")
+        nc.tensor.transpose(out=bias_bank[:], in_=bias_rows[:], identity=ident_bf16[:])
+        bias = const.tile([P, 2], F32)
+        nc.vector.tensor_copy(out=bias[:], in_=bias_bank[:, 0:2])
+        w_codes = const.tile([P, 2 * HIDDEN], U32, align_bytes=64)
+        w_scales = const.tile([P, 2 * HIDDEN], U8, align_bytes=64)
+        nc.vector.quantize_mx(
+            out=w_codes[:].bitcast(FP8X4),
+            scales=w_scales[:],
+            in_=w_grouped[:].rearrange("p o t -> p (o t)"),
+        )
+
+        x_grouped = {}
+        x_codes = {}
+        x_scales = {}
+
+        def regroup_x(piece):
+            grouped = x_stage.tile([P, CHANNELS, PACK], BF16, align_bytes=64)
+            nc.vector.tensor_copy(
+                out=grouped[:].rearrange("p (c i) t -> p c t i", i=4),
+                in_=x_raw[piece][:].rearrange("p t (c i) -> p c t i", i=4),
+            )
+            x_grouped[piece] = grouped
+
+        def quantise_x(piece):
+            b, s = divmod(piece, PASSES)
+            if s == 0:
+                codes = x_stage.tile([P, PASSES, CHANNELS], U32, align_bytes=64)
+                scales = x_stage.tile([P, PASSES, CHANNELS], U8, align_bytes=64)
+                x_codes[b] = codes
+                x_scales[b] = scales
+            nc.vector.quantize_mx(
+                out=x_codes[b][:, s, :].bitcast(FP8X4),
+                scales=x_scales[b][:, s, :],
+                in_=x_grouped[piece][:].rearrange("p c t -> p (c t)"),
+            )
+
+        regroup_x(0)
+        regroup_x(1)
+        quantise_x(0)
+        quantise_x(1)
+
+        a_codes = []
+        a_scales = []
+        for half in range(HALVES):
+            a_grouped = a_keep.tile([P, PASSES * HALF * PACK], BF16, align_bytes=64)
+            a_pairs = a_grouped[:].bitcast(F32).rearrange("p (s v u) -> p s v u", s=PASSES, u=2)
+            for k in range(BLOCKS):
+                a_words = a_raw[half * BLOCKS + k][:].bitcast(F32)
+                a_bank = psum_g.tile([P, PASSES * 2, P], F32, tag="g")
+                for su in range(PASSES * 2):
+                    nc.tensor.transpose(
+                        out=a_bank[:, su, :],
+                        in_=a_words[:, su * P : (su + 1) * P],
+                        identity=ident_f32[:],
+                    )
+                nc.scalar.copy(
+                    out=a_pairs[:, :, k * P : (k + 1) * P, :],
+                    in_=a_bank[:].rearrange("p (s u) v -> p s v u", u=2),
+                )
+            codes_half = a_keep.tile([P, PASSES, HALF], U32, align_bytes=64)
+            scales_half = a_keep.tile([P, PASSES, HALF], U8, align_bytes=64)
+            for s in range(PASSES):
+                nc.vector.quantize_mx(
+                    out=codes_half[:, s, :].bitcast(FP8X4),
+                    scales=scales_half[:, s, :],
+                    in_=a_grouped[:, s * HALF * PACK : (s + 1) * HALF * PACK],
+                )
+            a_codes.append(codes_half)
+            a_scales.append(scales_half)
+
+        regroup_x(2)
+
+        g_grouped = {}
+        g_codes = {}
+        g_scales = {}
+        gated = {}
+
+        def stage1(unit):
+            b, half = divmod(unit, HALVES)
+            grouped = g_stage.tile([P, HALF, PACK], BF16, align_bytes=64)
+            for k in range(BLOCKS):
+                g_bank = psum_g.tile([P, PACK, P], F32, tag="g")
+                for t in range(PACK):
+                    for s in range(PASSES):
+                        nc.tensor.matmul_mx(
+                            out=g_bank[:, t, :],
+                            lhsT=x_codes[b][:, s, t * P : (t + 1) * P].bitcast(FP8X4),
+                            lhsT_scale=x_scales[b][:, s, t * P : (t + 1) * P],
+                            rhs=a_codes[half][:, s, k * P : (k + 1) * P].bitcast(FP8X4),
+                            rhs_scale=a_scales[half][:, s, k * P : (k + 1) * P],
+                            start=(s == 0),
+                            stop=(s == PASSES - 1),
+                        )
+                nc.scalar.copy(
+                    out=grouped[:, k * P : (k + 1) * P, :], in_=g_bank[:].rearrange("p t v -> p v t")
+                )
+            g_grouped[unit] = grouped
+
+        def quantise_g(unit):
+            codes = g_stage.tile([P, HALF], U32, align_bytes=64)
+            scales = g_stage.tile([P, HALF], U8, align_bytes=64)
+            nc.vector.quantize_mx(
+                out=codes[:].bitcast(FP8X4),
+                scales=scales[:],
+                in_=g_grouped[unit][:].rearrange("p v t -> p (v t)"),
+            )
+            g_codes[unit] = codes
+            g_scales[unit] = scales
+
+        def stage2(unit):
+            y_banks = []
+            for h in (1, 0):
+                y_bank = psum_y.tile([P, HALF], F32, tag="y")
+                nc.tensor.matmul_mx(
+                    out=y_bank[:],
+                    lhsT=w_codes[:, h * HIDDEN : (h + 1) * HIDDEN].bitcast(FP8X4),
+                    lhsT_scale=w_scales[:, h * HIDDEN : (h + 1) * HIDDEN],
+                    rhs=g_codes[unit][:].bitcast(FP8X4),
+                    rhs_scale=g_scales[unit][:],
+                    start=True,
+                    stop=True,
+                )
+                y_banks.append(y_bank)
+            gate_bank, value_bank = y_banks
+            sig = glu.tile([P, HALF], F32)
+            nc.scalar.activation(
+                out=sig[:], in_=gate_bank[:], func=ACT.Sigmoid, bias=bias[:, 1:2], scale=1.0
+            )
+            product = glu.tile([P, HALF], F32)
+            nc.vector.scalar_tensor_tensor(
+                out=product[:],
+                in0=value_bank[:],
+                scalar=bias[:, 0:1],
+                in1=sig[:],
+                op0=ALU.add,
+                op1=ALU.mult,
+            )
+            gated[unit] = product
+
+        def write_out(b):
+            t_banks = []
+            for half in range(HALVES):
+                t_bank = psum_t.tile([P, BLOCKS, HIDDEN], F32, tag="t")
+                for k in range(BLOCKS):
+                    nc.tensor.transpose(
+                        out=t_bank[:, k, :],
+                        in_=gated[HALVES * b + half][:, k * P : (k + 1) * P],
+                        identity=ident_f32[:],
+                    )
+                t_banks.append(t_bank)
+            for half in range(HALVES):
+                result = glu.tile([P, BLOCKS, HIDDEN], F32)
+                if half == 0:
+                    nc.vector.tensor_copy(out=result[:], in_=t_banks[half][:])
+                else:
+                    nc.scalar.copy(out=result[:], in_=t_banks[half][:])
+                nc.sync.dma_start(
+                    out=out[half * HALF : (half + 1) * HALF, b, :].rearrange("(k p) j -> p k j", p=P),
+                    in_=result[:],
+                )
+
+        for step in range(UNITS + 2):
+            if step < UNITS:
+                stage1(step)
+            if 1 <= step <= UNITS:
+                quantise_g(step - 1)
+            if step + 2 < PIECES:
+                quantise_x(step + 2)
+            if step + 3 < PIECES:
+                regroup_x(step + 3)
+            if 1 <= step <= UNITS:
+                stage2(step - 1)
+            if step >= 3 and step % 2 == 1:
+                write_out((step - 3) // 2)

@@ -36,7 +36,7 @@ def tile_stsgcm_pa_t_kernel(tc, x, A, W0, b0, out):
         const = ctx.enter_context(tc.tile_pool(name="const", bufs=1))
         x_keep = ctx.enter_context(tc.tile_pool(name="x_keep", bufs=PIECES))
         a_load = ctx.enter_context(tc.tile_pool(name="a_load", bufs=HALVES * BLOCKS))
-        a_keep = ctx.enter_context(tc.tile_pool(name="a_keep", bufs=HALVES))
+        a_keep = ctx.enter_context(tc.tile_pool(name="a_keep", bufs=HALVES * BLOCKS))
         x_stage = ctx.enter_context(tc.tile_pool(name="x_stage", bufs=3))
         g_stage = ctx.enter_context(tc.tile_pool(name="g_stage", bufs=3))
         glu = ctx.enter_context(tc.tile_pool(name="glu", bufs=4))
@@ -129,18 +129,12 @@ def tile_stsgcm_pa_t_kernel(tc, x, A, W0, b0, out):
                 in_=x_grouped[piece][:].rearrange("p c t -> p (c t)"),
             )
 
-        regroup_x(0)
-        regroup_x(1)
-        quantise_x(0)
-        quantise_x(1)
+        a_codes = {}
+        a_scales = {}
 
-        a_codes = []
-        a_scales = []
-        for half in range(HALVES):
-            a_grouped = a_keep.tile([P, PASSES * HALF * PACK], BF16, align_bytes=64)
-            a_pairs = a_grouped[:].bitcast(F32).rearrange("p (s v u) -> p s v u", s=PASSES, u=2)
-            for k in range(BLOCKS):
-                a_words = a_raw[half * BLOCKS + k][:].bitcast(F32)
+        def prepare_a(half):
+            for block in range(half * BLOCKS, (half + 1) * BLOCKS):
+                a_words = a_raw[block][:].bitcast(F32)
                 a_bank = psum_g.tile([P, PASSES * 2, P], F32, tag="g")
                 for su in range(PASSES * 2):
                     nc.tensor.transpose(
@@ -148,22 +142,20 @@ def tile_stsgcm_pa_t_kernel(tc, x, A, W0, b0, out):
                         in_=a_words[:, su * P : (su + 1) * P],
                         identity=ident_f32[:],
                     )
+                a_grouped = a_keep.tile([P, PASSES * P * PACK], BF16, align_bytes=64)
                 nc.scalar.copy(
-                    out=a_pairs[:, :, k * P : (k + 1) * P, :],
+                    out=a_grouped[:].bitcast(F32).rearrange("p (s v u) -> p s v u", s=PASSES, u=2),
                     in_=a_bank[:].rearrange("p (s u) v -> p s v u", u=2),
                 )
-            codes_half = a_keep.tile([P, PASSES, HALF], U32, align_bytes=64)
-            scales_half = a_keep.tile([P, PASSES, HALF], U8, align_bytes=64)
-            for s in range(PASSES):
+                codes = a_keep.tile([P, PASSES, P], U32, align_bytes=64)
+                scales = a_keep.tile([P, PASSES, P], U8, align_bytes=64)
                 nc.vector.quantize_mx(
-                    out=codes_half[:, s, :].bitcast(FP8X4),
-                    scales=scales_half[:, s, :],
-                    in_=a_grouped[:, s * HALF * PACK : (s + 1) * HALF * PACK],
+                    out=codes[:].rearrange("p s v -> p (s v)").bitcast(FP8X4),
+                    scales=scales[:].rearrange("p s v -> p (s v)"),
+                    in_=a_grouped[:],
                 )
-            a_codes.append(codes_half)
-            a_scales.append(scales_half)
-
-        regroup_x(2)
+                a_codes[block] = codes
+                a_scales[block] = scales
 
         g_grouped = {}
         g_codes = {}
@@ -181,8 +173,8 @@ def tile_stsgcm_pa_t_kernel(tc, x, A, W0, b0, out):
                             out=g_bank[:, t, :],
                             lhsT=x_codes[b][:, s, t * P : (t + 1) * P].bitcast(FP8X4),
                             lhsT_scale=x_scales[b][:, s, t * P : (t + 1) * P],
-                            rhs=a_codes[half][:, s, k * P : (k + 1) * P].bitcast(FP8X4),
-                            rhs_scale=a_scales[half][:, s, k * P : (k + 1) * P],
+                            rhs=a_codes[half * BLOCKS + k][:, s, :].bitcast(FP8X4),
+                            rhs_scale=a_scales[half * BLOCKS + k][:, s, :],
                             start=(s == 0),
                             stop=(s == PASSES - 1),
                         )
@@ -254,15 +246,23 @@ def tile_stsgcm_pa_t_kernel(tc, x, A, W0, b0, out):
                     in_=result[:],
                 )
 
+        regroup_x(0)
+        regroup_x(1)
+        quantise_x(0)
+        quantise_x(1)
+        for half in range(HALVES):
+            prepare_a(half)
+        regroup_x(2)
+
         for step in range(UNITS + 2):
             if step < UNITS:
                 stage1(step)
-            if 1 <= step <= UNITS:
-                quantise_g(step - 1)
             if step + 2 < PIECES:
                 quantise_x(step + 2)
             if step + 3 < PIECES:
                 regroup_x(step + 3)
+            if step < UNITS:
+                quantise_g(step)
             if 1 <= step <= UNITS:
                 stage2(step - 1)
             if step >= 3 and step % 2 == 1:

@@ -11,21 +11,30 @@ FP8X4 = mybir.dt.float8_e4m3fn_x4
 ACT = mybir.ActivationFunctionType
 ALU = mybir.AluOpType
 
-P = 128
-PACK = 4
 NODES = 1024
 BATCH = 8
 CHANNELS = 512
 HIDDEN = 128
+PARTS = 2
+VALUE = 0
+GATE = 1
+
+P = 128
+PACK = 4
+PAIR = 2
+WORDS = PACK // PAIR
+MX_ALIGN = 64
 
 PASSES = NODES // (P * PACK)
+PIECES = BATCH * PASSES
+A_BLOCKS = NODES // P
 HALF = 512
 HALVES = NODES // HALF
 BLOCKS = HALF // P
 UNITS = BATCH * HALVES
-PIECES = BATCH * PASSES
+RUN = 4
 
-FLOPS = 2 * BATCH * CHANNELS * NODES * NODES + 2 * BATCH * 2 * HIDDEN * CHANNELS * NODES
+FLOPS = 2 * BATCH * CHANNELS * NODES * NODES + 2 * BATCH * PARTS * HIDDEN * CHANNELS * NODES
 
 
 def tile_stsgcm_pa_t_kernel(tc, x, A, W0, b0, out):
@@ -35,14 +44,14 @@ def tile_stsgcm_pa_t_kernel(tc, x, A, W0, b0, out):
 
         const = ctx.enter_context(tc.tile_pool(name="const", bufs=1))
         x_keep = ctx.enter_context(tc.tile_pool(name="x_keep", bufs=PIECES))
-        a_load = ctx.enter_context(tc.tile_pool(name="a_load", bufs=HALVES * BLOCKS))
-        a_keep = ctx.enter_context(tc.tile_pool(name="a_keep", bufs=HALVES * BLOCKS))
+        a_load = ctx.enter_context(tc.tile_pool(name="a_load", bufs=A_BLOCKS))
+        a_keep = ctx.enter_context(tc.tile_pool(name="a_keep", bufs=A_BLOCKS))
         x_stage = ctx.enter_context(tc.tile_pool(name="x_stage", bufs=3))
         g_stage = ctx.enter_context(tc.tile_pool(name="g_stage", bufs=3))
         glu = ctx.enter_context(tc.tile_pool(name="glu", bufs=4))
-        psum_g = ctx.enter_context(tc.psum_pool(name="psum_g", bufs=4))
-        psum_y = ctx.enter_context(tc.psum_pool(name="psum_y", bufs=2))
-        psum_t = ctx.enter_context(tc.psum_pool(name="psum_t", bufs=2))
+        psum_g = ctx.enter_context(tc.psum_pool(name="psum_g", bufs=BLOCKS))
+        psum_y = ctx.enter_context(tc.psum_pool(name="psum_y", bufs=PARTS))
+        psum_t = ctx.enter_context(tc.psum_pool(name="psum_t", bufs=HALVES))
 
         ident_f32 = const.tile([P, P], F32)
         make_identity(nc, ident_f32[:])
@@ -52,38 +61,38 @@ def tile_stsgcm_pa_t_kernel(tc, x, A, W0, b0, out):
         nc.vector.memset(bias_rows[:], 0.0)
         zero_col = const.tile([P, 1], F32)
         nc.vector.memset(zero_col[:], 0.0)
-        half_col = const.tile([P, 1], F32)
-        nc.scalar.activation(out=half_col[:], in_=zero_col[:], func=ACT.Sigmoid)
+        unused_col = const.tile([P, 1], F32)
+        nc.scalar.activation(out=unused_col[:], in_=zero_col[:], func=ACT.Sigmoid)
 
-        w_raw = const.tile([P, 2, CHANNELS], BF16)
-        nc.sync.dma_start(out=w_raw[:], in_=W0.rearrange("(h o) c -> o h c", h=2))
-        nc.sync.dma_start(out=bias_rows[0:2, :], in_=b0.rearrange("(h j) -> h j", h=2))
+        w_raw = const.tile([P, PARTS, CHANNELS], BF16)
+        nc.sync.dma_start(out=w_raw[:], in_=W0.rearrange("(h o) c -> o h c", h=PARTS))
+        nc.sync.dma_start(out=bias_rows[0:PARTS, :], in_=b0.rearrange("(h j) -> h j", h=PARTS))
 
         x_raw = {}
 
         def load_x(b):
             for s in range(PASSES):
                 x_piece = x_keep.tile([P, PACK, CHANNELS], BF16)
-                for u in range(2):
-                    first = s * P * PACK + u * 2 * P
+                for u in range(WORDS):
+                    first = s * P * PACK + u * P * PAIR
                     nc.sync.dma_start(
-                        out=x_piece[:, 2 * u : 2 * u + 2, :],
-                        in_=x[first : first + 2 * P, b, :].rearrange("(p e) c -> p e c", e=2),
+                        out=x_piece[:, PAIR * u : PAIR * (u + 1), :],
+                        in_=x[first : first + P * PAIR, b, :].rearrange("(p e) c -> p e c", e=PAIR),
                     )
                 x_raw[PASSES * b + s] = x_piece
 
         load_x(0)
         a_raw = []
-        for block in range(HALVES * BLOCKS):
+        for block in range(A_BLOCKS):
             a_rows = a_load.tile([P, NODES], BF16)
             nc.sync.dma_start(out=a_rows[:], in_=A[block * P : (block + 1) * P, :])
             a_raw.append(a_rows)
         for b in range(1, BATCH):
             load_x(b)
 
-        w_grouped = const.tile([P, 2 * HIDDEN, PACK], BF16, align_bytes=64)
-        for h in range(2):
-            w_bank = psum_t.tile([P, PACK, P], BF16, tag="t")
+        w_grouped = const.tile([P, PARTS * HIDDEN, PACK], BF16, align_bytes=MX_ALIGN)
+        for h in range(PARTS):
+            w_bank = psum_t.tile([P, PACK, HIDDEN], BF16, tag="t")
             for t in range(PACK):
                 nc.tensor.transpose(
                     out=w_bank[:, t, :], in_=w_raw[:, h, t * P : (t + 1) * P], identity=ident_bf16[:]
@@ -94,10 +103,10 @@ def tile_stsgcm_pa_t_kernel(tc, x, A, W0, b0, out):
             )
         bias_bank = psum_y.tile([P, P], BF16, tag="y")
         nc.tensor.transpose(out=bias_bank[:], in_=bias_rows[:], identity=ident_bf16[:])
-        bias = const.tile([P, 2], F32)
-        nc.vector.tensor_copy(out=bias[:], in_=bias_bank[:, 0:2])
-        w_codes = const.tile([P, 2 * HIDDEN], U32, align_bytes=64)
-        w_scales = const.tile([P, 2 * HIDDEN], U8, align_bytes=64)
+        bias = const.tile([P, PARTS], F32)
+        nc.vector.tensor_copy(out=bias[:], in_=bias_bank[:, 0:PARTS])
+        w_codes = const.tile([P, PARTS * HIDDEN], U32, align_bytes=MX_ALIGN)
+        w_scales = const.tile([P, PARTS * HIDDEN], U8, align_bytes=MX_ALIGN)
         nc.vector.quantize_mx(
             out=w_codes[:].bitcast(FP8X4),
             scales=w_scales[:],
@@ -109,20 +118,20 @@ def tile_stsgcm_pa_t_kernel(tc, x, A, W0, b0, out):
         x_scales = {}
 
         def regroup_x(piece):
-            grouped = x_stage.tile([P, CHANNELS, PACK], BF16, align_bytes=64)
+            piece_grouped = x_stage.tile([P, CHANNELS, PACK], BF16, align_bytes=MX_ALIGN)
             nc.vector.tensor_copy(
-                out=grouped[:].rearrange("p (c i) t -> p c t i", i=4),
-                in_=x_raw[piece][:].rearrange("p t (c i) -> p c t i", i=4),
+                out=piece_grouped[:].rearrange("p (c i) t -> p c t i", i=RUN),
+                in_=x_raw[piece][:].rearrange("p t (c i) -> p c t i", i=RUN),
             )
-            x_grouped[piece] = grouped
+            x_grouped[piece] = piece_grouped
 
         def quantise_x(piece):
             b, s = divmod(piece, PASSES)
             if s == 0:
-                codes = x_stage.tile([P, PASSES, CHANNELS], U32, align_bytes=64)
-                scales = x_stage.tile([P, PASSES, CHANNELS], U8, align_bytes=64)
-                x_codes[b] = codes
-                x_scales[b] = scales
+                batch_codes = x_stage.tile([P, PASSES, CHANNELS], U32, align_bytes=MX_ALIGN)
+                batch_scales = x_stage.tile([P, PASSES, CHANNELS], U8, align_bytes=MX_ALIGN)
+                x_codes[b] = batch_codes
+                x_scales[b] = batch_scales
             nc.vector.quantize_mx(
                 out=x_codes[b][:, s, :].bitcast(FP8X4),
                 scales=x_scales[b][:, s, :],
@@ -132,30 +141,27 @@ def tile_stsgcm_pa_t_kernel(tc, x, A, W0, b0, out):
         a_codes = {}
         a_scales = {}
 
-        def prepare_a(half):
-            for block in range(half * BLOCKS, (half + 1) * BLOCKS):
-                a_words = a_raw[block][:].bitcast(F32)
-                a_bank = psum_g.tile([P, PASSES * 2, P], F32, tag="g")
-                for su in range(PASSES * 2):
-                    nc.tensor.transpose(
-                        out=a_bank[:, su, :],
-                        in_=a_words[:, su * P : (su + 1) * P],
-                        identity=ident_f32[:],
-                    )
-                a_grouped = a_keep.tile([P, PASSES * P * PACK], BF16, align_bytes=64)
-                nc.scalar.copy(
-                    out=a_grouped[:].bitcast(F32).rearrange("p (s v u) -> p s v u", s=PASSES, u=2),
-                    in_=a_bank[:].rearrange("p (s u) v -> p s v u", u=2),
+        def prepare_a(block):
+            a_words = a_raw[block][:].bitcast(F32)
+            a_bank = psum_g.tile([P, PASSES * WORDS, P], F32, tag="g")
+            for su in range(PASSES * WORDS):
+                nc.tensor.transpose(
+                    out=a_bank[:, su, :], in_=a_words[:, su * P : (su + 1) * P], identity=ident_f32[:]
                 )
-                codes = a_keep.tile([P, PASSES, P], U32, align_bytes=64)
-                scales = a_keep.tile([P, PASSES, P], U8, align_bytes=64)
-                nc.vector.quantize_mx(
-                    out=codes[:].rearrange("p s v -> p (s v)").bitcast(FP8X4),
-                    scales=scales[:].rearrange("p s v -> p (s v)"),
-                    in_=a_grouped[:],
-                )
-                a_codes[block] = codes
-                a_scales[block] = scales
+            block_grouped = a_keep.tile([P, PASSES * P * PACK], BF16, align_bytes=MX_ALIGN)
+            nc.scalar.copy(
+                out=block_grouped[:].bitcast(F32).rearrange("p (s v u) -> p s v u", s=PASSES, u=WORDS),
+                in_=a_bank[:].rearrange("p (s u) v -> p s v u", u=WORDS),
+            )
+            block_codes = a_keep.tile([P, PASSES, P], U32, align_bytes=MX_ALIGN)
+            block_scales = a_keep.tile([P, PASSES, P], U8, align_bytes=MX_ALIGN)
+            nc.vector.quantize_mx(
+                out=block_codes[:].rearrange("p s v -> p (s v)").bitcast(FP8X4),
+                scales=block_scales[:].rearrange("p s v -> p (s v)"),
+                in_=block_grouped[:],
+            )
+            a_codes[block] = block_codes
+            a_scales[block] = block_scales
 
         g_grouped = {}
         g_codes = {}
@@ -164,8 +170,9 @@ def tile_stsgcm_pa_t_kernel(tc, x, A, W0, b0, out):
 
         def stage1(unit):
             b, half = divmod(unit, HALVES)
-            grouped = g_stage.tile([P, HALF, PACK], BF16, align_bytes=64)
+            unit_grouped = g_stage.tile([P, HALF, PACK], BF16, align_bytes=MX_ALIGN)
             for k in range(BLOCKS):
+                block = half * BLOCKS + k
                 g_bank = psum_g.tile([P, PACK, P], F32, tag="g")
                 for t in range(PACK):
                     for s in range(PASSES):
@@ -173,30 +180,31 @@ def tile_stsgcm_pa_t_kernel(tc, x, A, W0, b0, out):
                             out=g_bank[:, t, :],
                             lhsT=x_codes[b][:, s, t * P : (t + 1) * P].bitcast(FP8X4),
                             lhsT_scale=x_scales[b][:, s, t * P : (t + 1) * P],
-                            rhs=a_codes[half * BLOCKS + k][:, s, :].bitcast(FP8X4),
-                            rhs_scale=a_scales[half * BLOCKS + k][:, s, :],
+                            rhs=a_codes[block][:, s, :].bitcast(FP8X4),
+                            rhs_scale=a_scales[block][:, s, :],
                             start=(s == 0),
                             stop=(s == PASSES - 1),
                         )
                 nc.scalar.copy(
-                    out=grouped[:, k * P : (k + 1) * P, :], in_=g_bank[:].rearrange("p t v -> p v t")
+                    out=unit_grouped[:, k * P : (k + 1) * P, :],
+                    in_=g_bank[:].rearrange("p t v -> p v t"),
                 )
-            g_grouped[unit] = grouped
+            g_grouped[unit] = unit_grouped
 
         def quantise_g(unit):
-            codes = g_stage.tile([P, HALF], U32, align_bytes=64)
-            scales = g_stage.tile([P, HALF], U8, align_bytes=64)
+            unit_codes = g_stage.tile([P, HALF], U32, align_bytes=MX_ALIGN)
+            unit_scales = g_stage.tile([P, HALF], U8, align_bytes=MX_ALIGN)
             nc.vector.quantize_mx(
-                out=codes[:].bitcast(FP8X4),
-                scales=scales[:],
+                out=unit_codes[:].bitcast(FP8X4),
+                scales=unit_scales[:],
                 in_=g_grouped[unit][:].rearrange("p v t -> p (v t)"),
             )
-            g_codes[unit] = codes
-            g_scales[unit] = scales
+            g_codes[unit] = unit_codes
+            g_scales[unit] = unit_scales
 
         def stage2(unit):
-            y_banks = []
-            for h in (1, 0):
+            y_banks = {}
+            for h in (GATE, VALUE):
                 y_bank = psum_y.tile([P, HALF], F32, tag="y")
                 nc.tensor.matmul_mx(
                     out=y_bank[:],
@@ -207,17 +215,20 @@ def tile_stsgcm_pa_t_kernel(tc, x, A, W0, b0, out):
                     start=True,
                     stop=True,
                 )
-                y_banks.append(y_bank)
-            gate_bank, value_bank = y_banks
+                y_banks[h] = y_bank
             sig = glu.tile([P, HALF], F32)
             nc.scalar.activation(
-                out=sig[:], in_=gate_bank[:], func=ACT.Sigmoid, bias=bias[:, 1:2], scale=1.0
+                out=sig[:],
+                in_=y_banks[GATE][:],
+                func=ACT.Sigmoid,
+                bias=bias[:, GATE : GATE + 1],
+                scale=1.0,
             )
             product = glu.tile([P, HALF], F32)
             nc.vector.scalar_tensor_tensor(
                 out=product[:],
-                in0=value_bank[:],
-                scalar=bias[:, 0:1],
+                in0=y_banks[VALUE][:],
+                scalar=bias[:, VALUE : VALUE + 1],
                 in1=sig[:],
                 op0=ALU.add,
                 op1=ALU.mult,
@@ -250,8 +261,8 @@ def tile_stsgcm_pa_t_kernel(tc, x, A, W0, b0, out):
         regroup_x(1)
         quantise_x(0)
         quantise_x(1)
-        for half in range(HALVES):
-            prepare_a(half)
+        for block in range(A_BLOCKS):
+            prepare_a(block)
         regroup_x(2)
 
         for step in range(UNITS + 2):
@@ -265,5 +276,6 @@ def tile_stsgcm_pa_t_kernel(tc, x, A, W0, b0, out):
                 quantise_g(step)
             if 1 <= step <= UNITS:
                 stage2(step - 1)
-            if step >= 3 and step % 2 == 1:
-                write_out((step - 3) // 2)
+            gated_before = step - 2
+            if gated_before >= 0 and gated_before % HALVES == HALVES - 1:
+                write_out(gated_before // HALVES)

@@ -40,8 +40,6 @@ FLOPS = 2 * BATCH * CHANNELS * NODES * NODES + 2 * BATCH * PARTS * HIDDEN * CHAN
 def tile_stsgcm_pa_t_kernel(tc, x, A, W0, b0, out):
     nc = tc.nc
     with ExitStack() as ctx:
-        ctx.enter_context(tc.manual_schedule())
-
         const = ctx.enter_context(tc.tile_pool(name="const", bufs=1))
         x_keep = ctx.enter_context(tc.tile_pool(name="x_keep", bufs=PIECES))
         a_load = ctx.enter_context(tc.tile_pool(name="a_load", bufs=A_BLOCKS))

from contextlib import ExitStack

import concourse.mybir as mybir
from concourse.masks import make_identity

F32 = mybir.dt.float32
BF16 = mybir.dt.bfloat16
U32 = mybir.dt.uint32
U8 = mybir.dt.uint8
FP8X4 = mybir.dt.float8_e4m3fn_x4
ACT = mybir.ActivationFunctionType
ALU = mybir.AluOpType

NODES = 1024
BATCH = 8
CHANNELS = 512
HIDDEN = 128
PARTS = 2
VALUE = 0
GATE = 1

P = 128
PACK = 4
PAIR = 2
WORDS = PACK // PAIR
MX_ALIGN = 64

PASSES = NODES // (P * PACK)
PIECES = BATCH * PASSES
A_BLOCKS = NODES // P
HALF = 512
HALVES = NODES // HALF
BLOCKS = HALF // P
UNITS = BATCH * HALVES
RUN = 4

FLOPS = 2 * BATCH * CHANNELS * NODES * NODES + 2 * BATCH * PARTS * HIDDEN * CHANNELS * NODES


def tile_stsgcm_pa_t_kernel(tc, x, A, W0, b0, out):
    nc = tc.nc
    with ExitStack() as ctx:
        const = ctx.enter_context(tc.tile_pool(name="const", bufs=1))
        x_keep = ctx.enter_context(tc.tile_pool(name="x_keep", bufs=PIECES))
        a_load = ctx.enter_context(tc.tile_pool(name="a_load", bufs=A_BLOCKS))
        a_keep = ctx.enter_context(tc.tile_pool(name="a_keep", bufs=A_BLOCKS))
        x_stage = ctx.enter_context(tc.tile_pool(name="x_stage", bufs=3))
        g_stage = ctx.enter_context(tc.tile_pool(name="g_stage", bufs=3))
        glu = ctx.enter_context(tc.tile_pool(name="glu", bufs=4))
        psum_g = ctx.enter_context(tc.psum_pool(name="psum_g", bufs=BLOCKS))
        psum_y = ctx.enter_context(tc.psum_pool(name="psum_y", bufs=PARTS))
        psum_t = ctx.enter_context(tc.psum_pool(name="psum_t", bufs=HALVES))

        ident_f32 = const.tile([P, P], F32)
        make_identity(nc, ident_f32[:])
        ident_bf16 = const.tile([P, P], BF16)
        make_identity(nc, ident_bf16[:])
        bias_rows = const.tile([P, P], BF16)
        nc.vector.memset(bias_rows[:], 0.0)
        zero_col = const.tile([P, 1], F32)
        nc.vector.memset(zero_col[:], 0.0)
        unused_col = const.tile([P, 1], F32)
        nc.scalar.activation(out=unused_col[:], in_=zero_col[:], func=ACT.Sigmoid)

        w_raw = const.tile([P, PARTS, CHANNELS], BF16)
        nc.sync.dma_start(out=w_raw[:], in_=W0.rearrange("(h o) c -> o h c", h=PARTS))
        nc.sync.dma_start(out=bias_rows[0:PARTS, :], in_=b0.rearrange("(h j) -> h j", h=PARTS))

        x_raw = {}

        def load_x(b):
            for s in range(PASSES):
                x_piece = x_keep.tile([P, PACK, CHANNELS], BF16)
                for u in range(WORDS):
                    first = s * P * PACK + u * P * PAIR
                    nc.sync.dma_start(
                        out=x_piece[:, PAIR * u : PAIR * (u + 1), :],
                        in_=x[first : first + P * PAIR, b, :].rearrange("(p e) c -> p e c", e=PAIR),
                    )
                x_raw[PASSES * b + s] = x_piece

        load_x(0)
        a_raw = []
        for block in range(A_BLOCKS):
            a_rows = a_load.tile([P, NODES], BF16)
            nc.sync.dma_start(out=a_rows[:], in_=A[block * P : (block + 1) * P, :])
            a_raw.append(a_rows)
        for b in range(1, BATCH):
            load_x(b)

        w_grouped = const.tile([P, PARTS * HIDDEN, PACK], BF16, align_bytes=MX_ALIGN)
        for h in range(PARTS):
            w_bank = psum_t.tile([P, PACK, HIDDEN], BF16, tag="t")
            for t in range(PACK):
                nc.tensor.transpose(
                    out=w_bank[:, t, :], in_=w_raw[:, h, t * P : (t + 1) * P], identity=ident_bf16[:]
                )
            nc.vector.tensor_copy(
                out=w_grouped[:, h * HIDDEN : (h + 1) * HIDDEN, :],
                in_=w_bank[:].rearrange("p t o -> p o t"),
            )
        bias_bank = psum_y.tile([P, P], BF16, tag="y")
        nc.tensor.transpose(out=bias_bank[:], in_=bias_rows[:], identity=ident_bf16[:])
        bias = const.tile([P, PARTS], F32)
        nc.vector.tensor_copy(out=bias[:], in_=bias_bank[:, 0:PARTS])
        w_codes = const.tile([P, PARTS * HIDDEN], U32, align_bytes=MX_ALIGN)
        w_scales = const.tile([P, PARTS * HIDDEN], U8, align_bytes=MX_ALIGN)
        nc.vector.quantize_mx(
            out=w_codes[:].bitcast(FP8X4),
            scales=w_scales[:],
            in_=w_grouped[:].rearrange("p o t -> p (o t)"),
        )

        x_grouped = {}
        x_codes = {}
        x_scales = {}

        def regroup_x(piece):
            piece_grouped = x_stage.tile([P, CHANNELS, PACK], BF16, align_bytes=MX_ALIGN)
            nc.vector.tensor_copy(
                out=piece_grouped[:].rearrange("p (c i) t -> p c t i", i=RUN),
                in_=x_raw[piece][:].rearrange("p t (c i) -> p c t i", i=RUN),
            )
            x_grouped[piece] = piece_grouped

        def quantise_x(piece):
            b, s = divmod(piece, PASSES)
            if s == 0:
                batch_codes = x_stage.tile([P, PASSES, CHANNELS], U32, align_bytes=MX_ALIGN)
                batch_scales = x_stage.tile([P, PASSES, CHANNELS], U8, align_bytes=MX_ALIGN)
                x_codes[b] = batch_codes
                x_scales[b] = batch_scales
            nc.vector.quantize_mx(
                out=x_codes[b][:, s, :].bitcast(FP8X4),
                scales=x_scales[b][:, s, :],
                in_=x_grouped[piece][:].rearrange("p c t -> p (c t)"),
            )

        a_codes = {}
        a_scales = {}

        def prepare_a(block):
            a_words = a_raw[block][:].bitcast(F32)
            a_bank = psum_g.tile([P, PASSES * WORDS, P], F32, tag="g")
            for su in range(PASSES * WORDS):
                nc.tensor.transpose(
                    out=a_bank[:, su, :], in_=a_words[:, su * P : (su + 1) * P], identity=ident_f32[:]
                )
            block_grouped = a_keep.tile([P, PASSES * P * PACK], BF16, align_bytes=MX_ALIGN)
            nc.scalar.copy(
                out=block_grouped[:].bitcast(F32).rearrange("p (s v u) -> p s v u", s=PASSES, u=WORDS),
                in_=a_bank[:].rearrange("p (s u) v -> p s v u", u=WORDS),
            )
            block_codes = a_keep.tile([P, PASSES, P], U32, align_bytes=MX_ALIGN)
            block_scales = a_keep.tile([P, PASSES, P], U8, align_bytes=MX_ALIGN)
            nc.vector.quantize_mx(
                out=block_codes[:].rearrange("p s v -> p (s v)").bitcast(FP8X4),
                scales=block_scales[:].rearrange("p s v -> p (s v)"),
                in_=block_grouped[:],
            )
            a_codes[block] = block_codes
            a_scales[block] = block_scales

        g_grouped = {}
        g_codes = {}
        g_scales = {}
        gated = {}

        def stage1(unit):
            b, half = divmod(unit, HALVES)
            unit_grouped = g_stage.tile([P, HALF, PACK], BF16, align_bytes=MX_ALIGN)
            for k in range(BLOCKS):
                block = half * BLOCKS + k
                g_bank = psum_g.tile([P, PACK, P], F32, tag="g")
                for t in range(PACK):
                    for s in range(PASSES):
                        nc.tensor.matmul_mx(
                            out=g_bank[:, t, :],
                            lhsT=x_codes[b][:, s, t * P : (t + 1) * P].bitcast(FP8X4),
                            lhsT_scale=x_scales[b][:, s, t * P : (t + 1) * P],
                            rhs=a_codes[block][:, s, :].bitcast(FP8X4),
                            rhs_scale=a_scales[block][:, s, :],
                            start=(s == 0),
                            stop=(s == PASSES - 1),
                        )
                nc.scalar.copy(
                    out=unit_grouped[:, k * P : (k + 1) * P, :],
                    in_=g_bank[:].rearrange("p t v -> p v t"),
                )
            g_grouped[unit] = unit_grouped

        def quantise_g(unit):
            unit_codes = g_stage.tile([P, HALF], U32, align_bytes=MX_ALIGN)
            unit_scales = g_stage.tile([P, HALF], U8, align_bytes=MX_ALIGN)
            nc.vector.quantize_mx(
                out=unit_codes[:].bitcast(FP8X4),
                scales=unit_scales[:],
                in_=g_grouped[unit][:].rearrange("p v t -> p (v t)"),
            )
            g_codes[unit] = unit_codes
            g_scales[unit] = unit_scales

        def stage2(unit):
            y_banks = {}
            for h in (GATE, VALUE):
                y_bank = psum_y.tile([P, HALF], F32, tag="y")
                nc.tensor.matmul_mx(
                    out=y_bank[:],
                    lhsT=w_codes[:, h * HIDDEN : (h + 1) * HIDDEN].bitcast(FP8X4),
                    lhsT_scale=w_scales[:, h * HIDDEN : (h + 1) * HIDDEN],
                    rhs=g_codes[unit][:].bitcast(FP8X4),
                    rhs_scale=g_scales[unit][:],
                    start=True,
                    stop=True,
                )
                y_banks[h] = y_bank
            sig = glu.tile([P, HALF], F32)
            nc.scalar.activation(
                out=sig[:],
                in_=y_banks[GATE][:],
                func=ACT.Sigmoid,
                bias=bias[:, GATE : GATE + 1],
                scale=1.0,
            )
            product = glu.tile([P, HALF], F32)
            nc.vector.scalar_tensor_tensor(
                out=product[:],
                in0=y_banks[VALUE][:],
                scalar=bias[:, VALUE : VALUE + 1],
                in1=sig[:],
                op0=ALU.add,
                op1=ALU.mult,
            )
            gated[unit] = product

        def write_out(b):
            t_banks = []
            for half in range(HALVES):
                t_bank = psum_t.tile([P, BLOCKS, HIDDEN], F32, tag="t")
                for k in range(BLOCKS):
                    nc.tensor.transpose(
                        out=t_bank[:, k, :],
                        in_=gated[HALVES * b + half][:, k * P : (k + 1) * P],
                        identity=ident_f32[:],
                    )
                t_banks.append(t_bank)
            for half in range(HALVES):
                result = glu.tile([P, BLOCKS, HIDDEN], F32)
                if half == 0:
                    nc.vector.tensor_copy(out=result[:], in_=t_banks[half][:])
                else:
                    nc.scalar.copy(out=result[:], in_=t_banks[half][:])
                nc.sync.dma_start(
                    out=out[half * HALF : (half + 1) * HALF, b, :].rearrange("(k p) j -> p k j", p=P),
                    in_=result[:],
                )

        regroup_x(0)
        regroup_x(1)
        quantise_x(0)
        quantise_x(1)
        for block in range(A_BLOCKS):
            prepare_a(block)
        regroup_x(2)

        for step in range(UNITS + 2):
            if step < UNITS:
                stage1(step)
            if step + 2 < PIECES:
                quantise_x(step + 2)
            if step + 3 < PIECES:
                regroup_x(step + 3)
            if step < UNITS:
                quantise_g(step)
            if 1 <= step <= UNITS:
                stage2(step - 1)
            gated_before = step - 2
            if gated_before >= 0 and gated_before % HALVES == HALVES - 1:
                write_out(gated_before // HALVES)
